import numpy as np
import ml_dtypes


def mxq(x, axis, fmt="e4m3"):
    dtype, down = {"e4m3": (ml_dtypes.float8_e4m3fn, 7), "e5m2": (ml_dtypes.float8_e5m2, 14)}[fmt]
    v = np.moveaxis(np.asarray(x, np.float32).astype(ml_dtypes.bfloat16).astype(np.float64), axis, -1)
    blocks = v.reshape(v.shape[:-1] + (-1, 32))
    amax = np.abs(blocks).max(-1, keepdims=True)
    byte = np.maximum(np.where(amax > 0, np.frexp(amax)[1] - 1 + 127, 0) - down, 1)
    scale = np.exp2(byte - 127.0)
    codes = (blocks / scale).astype(np.float32).astype(dtype).astype(np.float64)
    return np.moveaxis((codes * scale).reshape(v.shape), -1, axis)


WIDE = False


def mx_kscale(k):
    if not WIDE:
        return np.ones(k)
    levels = np.array([10, -10, 5, -5, 0])
    a = np.random.permutation(np.resize(levels, k // 512 * 4)).reshape(k // 512, 4)
    idx = np.arange(k)
    return np.exp2(a[idx // 512, idx % 128 // 32])


BF16 = ml_dtypes.bfloat16


def bf(x):
    return np.asarray(x, np.float32).astype(BF16)


def f64(x):
    return np.asarray(x).astype(np.float64)


B, T, D, A, H, E = 4, 512, 1024, 1024, 4, 2048
DH = A // H
EPS = 1e-5


def layernorm(v, w, b):
    mu = v.mean(-1, keepdims=True)
    var = np.square(v - mu).mean(-1, keepdims=True)
    return (v - mu) / np.sqrt(var + EPS) * w + b


def setup_inputs():
    s = mx_kscale(D)
    return {'x': bf(np.random.standard_normal((B, T, D))),
            'ln_w': bf((1.0 + 0.1 * np.random.standard_normal(D)) * s),
            'ln_b': bf(0.1 * np.random.standard_normal(D) * s),
            'q_w': bf(np.random.standard_normal((D, A)) * 1.5 / np.sqrt(D) / s[:, None]),
            'q_b': bf(np.random.standard_normal(A) * 0.3)}


def reference(x, ln_w, ln_b, q_w, q_b):
    xn = layernorm(f64(x), f64(ln_w), f64(ln_b))
    q = (mxq(xn, 2, 'e4m3') @ mxq(f64(q_w), 0, 'e4m3')) + f64(q_b)
    q = q.reshape(B, T, H, DH)
    e = np.exp(q - q.max(-1, keepdims=True))
    return (e / e.sum(-1, keepdims=True)).reshape(B, T, A)

@@ -1,0 +1,273 @@
+from contextlib import ExitStack
+
+import concourse.mybir as mybir
+from concourse.masks import make_identity
+
+F32 = mybir.dt.float32
+BF16 = mybir.dt.bfloat16
+U32 = mybir.dt.uint32
+U8 = mybir.dt.uint8
+FP8X4 = mybir.dt.float8_e4m3fn_x4
+ALU = mybir.AluOpType
+ACT = mybir.ActivationFunctionType
+AXIS = mybir.AxisListType
+
+P = 128
+TOKENS = 4 * 512
+D = 1024
+A = 1024
+HEADS = 4
+HEAD_COLS = A // HEADS
+EPS = 1e-5
+
+PACK = 4
+K_PASS = P * PACK
+PASSES = D // K_PASS
+CHUNKS = D // P
+SUBTILES = 2
+BLOCK = P * SUBTILES
+BLOCKS = TOKENS // BLOCK
+BANK = 512
+HALVES = A // BANK
+STAT_COLS = 512
+STAT_DIM = 6
+
+LEAD_STATS = 4
+LEAD_CENTRE = 3
+LEAD_TRANSPOSE = 2
+LEAD_MATMUL = 1
+WEIGHTS_BEFORE_STEP = -1
+
+FLOPS = 2 * TOKENS * D * A
+
+
+def tile_efficientcrossattention_pa_kernel(tc, x, ln_w, ln_b, q_w, q_b, out):
+    nc = tc.nc
+    x_blocks = x.flatten_outer_dims().rearrange("(b p i) k -> b p i k", p=P, i=SUBTILES)
+    out_blocks = out.flatten_outer_dims().rearrange("(b p i) a -> b p i a", p=P, i=SUBTILES)
+
+    with ExitStack() as ctx:
+        const = ctx.enter_context(tc.tile_pool(name="const", bufs=1))
+        x_pool = ctx.enter_context(tc.tile_pool(name="x", bufs=BLOCKS))
+        norm_pool = ctx.enter_context(tc.tile_pool(name="norm", bufs=3))
+        small = ctx.enter_context(tc.tile_pool(name="small", bufs=8))
+        soft_pool = ctx.enter_context(tc.tile_pool(name="soft", bufs=4))
+        psum_t = ctx.enter_context(tc.psum_pool(name="psum_t", bufs=4))
+        psum_q = ctx.enter_context(tc.psum_pool(name="psum_q", bufs=4))
+        ctx.enter_context(tc.manual_schedule())
+
+        x_tiles = []
+        for b in range(BLOCKS):
+            x_blk = x_pool.tile([P, SUBTILES, D], BF16)
+            x_tiles.append(x_blk)
+        w_raw = const.tile([P, PASSES, PACK, A], BF16)
+        w_view = q_w.rearrange("(g j p) n -> g p j n", j=PACK, p=P)
+        rows_bf = const.tile([P, P], BF16)
+        nc.vector.memset(rows_bf[:], 0.0)
+        nc.sync.dma_start(out=rows_bf[0:CHUNKS, :], in_=ln_w.rearrange("(c p) -> c p", p=P))
+        nc.sync.dma_start(out=rows_bf[CHUNKS : 2 * CHUNKS, :], in_=ln_b.rearrange("(c p) -> c p", p=P))
+        for b in range(2):
+            nc.sync.dma_start(out=x_tiles[b][:], in_=x_blocks[b])
+        bias_bc = const.tile([P, A], BF16)
+        nc.sync.dma_start(out=bias_bc[:], in_=q_b.partition_broadcast(P))
+        for g in range(PASSES):
+            nc.sync.dma_start(out=w_raw[:, g], in_=w_view[g])
+        for b in range(2, BLOCKS):
+            nc.sync.dma_start(out=x_tiles[b][:], in_=x_blocks[b])
+
+        ident = const.tile([P, P], F32)
+        make_identity(nc, ident[:])
+        neg_half = const.tile([P, SUBTILES], F32)
+        nc.vector.memset(neg_half[:], -0.5)
+        rows_f = const.tile([P, P], F32)
+        nc.vector.tensor_copy(out=rows_f[:], in_=rows_bf[:])
+        rows_t = psum_t.tile([P, BANK], F32, tag="bank")
+        nc.tensor.transpose(rows_t[:, 0:P], rows_f[:], ident[:])
+        affine = const.tile([P, 2 * CHUNKS], F32)
+        nc.vector.tensor_copy(out=affine[:], in_=rows_t[:, 0 : 2 * CHUNKS])
+
+        w_grouped = const.tile([P, PASSES, A, PACK], BF16, align_bytes=64)
+        w_codes = const.tile([P, PASSES, A], U32, align_bytes=64)
+        w_scales = const.tile([P, PASSES, A], U8, align_bytes=64)
+
+        def quantise_weights():
+            for g in range(PASSES):
+                for n in range(HALVES):
+                    cols = slice(n * BANK, (n + 1) * BANK)
+                    nc.vector.tensor_copy(
+                        out=w_grouped[:, g, cols, :].rearrange("p (c i) j -> p c j i", i=4),
+                        in_=w_raw[:, g, :, cols].rearrange("p j (c i) -> p c j i", i=4),
+                    )
+            for g in range(PASSES):
+                for n in range(HALVES):
+                    cols = slice(n * BANK, (n + 1) * BANK)
+                    nc.vector.quantize_mx(
+                        out=w_codes[:, g, cols].bitcast(FP8X4),
+                        scales=w_scales[:, g, cols],
+                        in_=w_grouped[:, g, cols, :].rearrange("p n j -> p (n j)"),
+                    )
+
+        moments = {}
+        x_hats = {}
+        groupeds = {}
+        operands = {}
+        accs = {}
+        logit_tiles = {}
+        expo_tiles = {}
+
+        def stats(b):
+            mean_var = small.tile([P, SUBTILES, 2], F32)
+            for i in range(SUBTILES):
+                stat = small.tile([P, (D // STAT_COLS) * STAT_DIM], F32)
+                for h in range(D // STAT_COLS):
+                    nc.vector.bn_stats(
+                        out=stat[:, h * STAT_DIM : (h + 1) * STAT_DIM],
+                        in_=x_tiles[b][:, i, h * STAT_COLS : (h + 1) * STAT_COLS],
+                    )
+                nc.vector.bn_aggr(out=mean_var[:, i, :], in_=stat[:])
+            neg_mean = small.tile([P, SUBTILES], F32)
+            nc.vector.tensor_scalar_mul(out=neg_mean[:], in0=mean_var[:, :, 0], scalar1=-1.0)
+            var_eps = small.tile([P, SUBTILES], F32)
+            nc.vector.tensor_scalar_add(out=var_eps[:], in0=mean_var[:, :, 1], scalar1=EPS)
+            rstd = small.tile([P, SUBTILES], F32)
+            nc.gpsimd.tensor_tensor(out=rstd[:], in0=var_eps[:], in1=neg_half[:], op=ALU.pow)
+            moments[b] = (neg_mean, rstd)
+
+        def centre(b):
+            neg_mean, rstd = moments[b]
+            x_hat = norm_pool.tile([P, SUBTILES, D], F32)
+            for i in range(SUBTILES):
+                nc.gpsimd.tensor_scalar(
+                    out=x_hat[:, i, :],
+                    in0=x_tiles[b][:, i, :],
+                    scalar1=neg_mean[:, i : i + 1],
+                    scalar2=rstd[:, i : i + 1],
+                    op0=ALU.add,
+                    op1=ALU.mult,
+                )
+            x_hats[b] = x_hat
+
+        def transpose_affine(b):
+            x_hat = x_hats[b]
+            planes = norm_pool.tile([P, CHUNKS, BLOCK], BF16)
+            grouped = norm_pool.tile([P, PASSES, BLOCK, PACK], BF16, align_bytes=64)
+            for g in range(PASSES):
+                for j in range(PACK):
+                    c = g * PACK + j
+                    bank = psum_t.tile([P, BANK], F32, tag="bank")
+                    for i in range(SUBTILES):
+                        nc.tensor.transpose(
+                            bank[:, i * P : (i + 1) * P], x_hat[:, i, c * P : (c + 1) * P], ident[:]
+                        )
+                    nc.scalar.activation(
+                        out=planes[:, c, :],
+                        in_=bank[:, 0:BLOCK],
+                        func=ACT.Identity,
+                        scale=affine[:, c : c + 1],
+                        bias=affine[:, CHUNKS + c : CHUNKS + c + 1],
+                    )
+                nc.scalar.copy(
+                    out=grouped[:, g].rearrange("p (c i) j -> p c j i", i=4),
+                    in_=planes[:, g * PACK : (g + 1) * PACK, :].rearrange("p j (c i) -> p c j i", i=4),
+                )
+            groupeds[b] = grouped
+
+        def quantise(b):
+            grouped = groupeds[b]
+            x_codes = norm_pool.tile([P, PASSES, BLOCK], U32, align_bytes=64)
+            x_scales = norm_pool.tile([P, PASSES, BLOCK], U8, align_bytes=64)
+            for g in range(PASSES):
+                nc.vector.quantize_mx(
+                    out=x_codes[:, g, :].bitcast(FP8X4),
+                    scales=x_scales[:, g, :],
+                    in_=grouped[:, g].rearrange("p t j -> p (t j)"),
+                )
+            operands[b] = (x_codes, x_scales)
+
+        def matmuls(b):
+            x_codes, x_scales = operands[b]
+            for i in range(SUBTILES):
+                tok = slice(i * P, (i + 1) * P)
+                for n in range(HALVES):
+                    cols = slice(n * BANK, (n + 1) * BANK)
+                    acc = psum_q.tile([P, BANK], F32)
+                    for g in range(PASSES):
+                        nc.tensor.matmul_mx(
+                            out=acc[:],
+                            lhsT=x_codes[:, g, tok].bitcast(FP8X4),
+                            lhsT_scale=x_scales[:, g, tok],
+                            rhs=w_codes[:, g, cols].bitcast(FP8X4),
+                            rhs_scale=w_scales[:, g, cols],
+                            start=(g == 0),
+                            stop=(g == PASSES - 1),
+                        )
+                    accs[(b, i, n)] = acc
+
+        def bias_max(b):
+            for i in range(SUBTILES):
+                logits = soft_pool.tile([P, A], F32)
+                for n in range(HALVES):
+                    cols = slice(n * BANK, (n + 1) * BANK)
+                    nc.vector.tensor_tensor(
+                        out=logits[:, cols], in0=accs[(b, i, n)][:], in1=bias_bc[:, cols], op=ALU.add
+                    )
+                neg_max = small.tile([P, HEADS], F32)
+                nc.vector.tensor_reduce(
+                    out=neg_max[:],
+                    in_=logits[:].rearrange("p (h d) -> p h d", h=HEADS),
+                    axis=AXIS.X,
+                    op=ALU.max,
+                    negate=True,
+                )
+                logit_tiles[(b, i)] = (logits, neg_max)
+
+        def exponentials(b):
+            for i in range(SUBTILES):
+                logits, neg_max = logit_tiles[(b, i)]
+                expo = soft_pool.tile([P, A], F32)
+                sums = small.tile([P, HEADS], F32)
+                for h in range(HEADS):
+                    head = slice(h * HEAD_COLS, (h + 1) * HEAD_COLS)
+                    nc.scalar.activation(
+                        out=expo[:, head],
+                        in_=logits[:, head],
+                        func=ACT.Exp,
+                        bias=neg_max[:, h : h + 1],
+                        scale=1.0,
+                        accum_out=sums[:, h : h + 1],
+                    )
+                expo_tiles[(b, i)] = (expo, sums)
+
+        def finish(b):
+            for i in range(SUBTILES):
+                expo, sums = expo_tiles[(b, i)]
+                inv_sums = small.tile([P, HEADS], F32)
+                nc.vector.reciprocal(out=inv_sums[:], in_=sums[:])
+                probs = soft_pool.tile([P, A], F32)
+                for h in range(HEADS):
+                    head = slice(h * HEAD_COLS, (h + 1) * HEAD_COLS)
+                    nc.gpsimd.tensor_scalar(
+                        out=probs[:, head],
+                        in0=expo[:, head],
+                        scalar1=inv_sums[:, h : h + 1],
+                        scalar2=1.0,
+                        op0=ALU.mult,
+                        op1=ALU.mult,
+                    )
+                nc.sync.dma_start(out=out_blocks[b][:, i, :], in_=probs[:])
+
+        def run(stage, b):
+            if 0 <= b < BLOCKS:
+                stage(b)
+
+        for step in range(-LEAD_STATS, BLOCKS + 1):
+            if step == WEIGHTS_BEFORE_STEP:
+                quantise_weights()
+            run(transpose_affine, step + LEAD_TRANSPOSE)
+            run(centre, step + LEAD_CENTRE)
+            run(quantise, step + LEAD_MATMUL)
+            run(matmuls, step + LEAD_MATMUL)
+            run(bias_max, step)
+            run(exponentials, step)
+            run(finish, step - 1)
+            run(stats, step + LEAD_STATS)

@@ -24,6 +24,7 @@ PACK = 4
 K_PASS = P * PACK
 PASSES = D // K_PASS
 CHUNKS = D // P
+TILES = TOKENS // P
 SUBTILES = 2
 BLOCK = P * SUBTILES
 BLOCKS = TOKENS // BLOCK
@@ -32,11 +33,17 @@ HALVES = A // BANK
 STAT_COLS = 512
 STAT_DIM = 6
 
-LEAD_STATS = 4
-LEAD_CENTRE = 3
-LEAD_TRANSPOSE = 2
-LEAD_MATMUL = 1
-WEIGHTS_BEFORE_STEP = -1
+assert SUBTILES == PASSES
+LEAD_STATS = 10
+LEAD_MOMENTS = 9
+LEAD_CENTRE = 8
+LEAD_TRANSPOSE = 5
+LEAD_QUANTISE = 3
+LEAD_MATMUL = 2
+LEAD_BIAS = 1
+LAG_EXP = 1
+LAG_SCALE = 2
+WEIGHTS_STEP = -4
 
 FLOPS = 2 * TOKENS * D * A
 
@@ -49,27 +56,29 @@ def tile_efficientcrossattention_pa_kernel(tc, x, ln_w, ln_b, q_w, q_b, out):
     with ExitStack() as ctx:
         const = ctx.enter_context(tc.tile_pool(name="const", bufs=1))
         x_pool = ctx.enter_context(tc.tile_pool(name="x", bufs=BLOCKS))
-        norm_pool = ctx.enter_context(tc.tile_pool(name="norm", bufs=3))
-        small = ctx.enter_context(tc.tile_pool(name="small", bufs=8))
+        hat_pool = ctx.enter_context(tc.tile_pool(name="hat", bufs=6))
+        norm_pool = ctx.enter_context(tc.tile_pool(name="norm", bufs=4))
+        code_pool = ctx.enter_context(tc.tile_pool(name="code", bufs=6))
+        small = ctx.enter_context(tc.tile_pool(name="small", bufs=16))
         soft_pool = ctx.enter_context(tc.tile_pool(name="soft", bufs=4))
         psum_t = ctx.enter_context(tc.psum_pool(name="psum_t", bufs=4))
         psum_q = ctx.enter_context(tc.psum_pool(name="psum_q", bufs=4))
         ctx.enter_context(tc.manual_schedule())
 
-        x_tiles = []
-        for b in range(BLOCKS):
-            x_blk = x_pool.tile([P, SUBTILES, D], BF16)
-            x_tiles.append(x_blk)
-        w_raw = const.tile([P, PASSES, PACK, A], BF16)
-        w_view = q_w.rearrange("(g j p) n -> g p j n", j=PACK, p=P)
         rows_bf = const.tile([P, P], BF16)
         nc.vector.memset(rows_bf[:], 0.0)
         nc.sync.dma_start(out=rows_bf[0:CHUNKS, :], in_=ln_w.rearrange("(c p) -> c p", p=P))
         nc.sync.dma_start(out=rows_bf[CHUNKS : 2 * CHUNKS, :], in_=ln_b.rearrange("(c p) -> c p", p=P))
+        x_tiles = []
+        for b in range(BLOCKS):
+            x_blk = x_pool.tile([P, SUBTILES, D], BF16)
+            x_tiles.append(x_blk)
         for b in range(2):
             nc.sync.dma_start(out=x_tiles[b][:], in_=x_blocks[b])
         bias_bc = const.tile([P, A], BF16)
         nc.sync.dma_start(out=bias_bc[:], in_=q_b.partition_broadcast(P))
+        w_raw = const.tile([P, PASSES, PACK, A], BF16)
+        w_view = q_w.rearrange("(g j p) n -> g p j n", j=PACK, p=P)
         for g in range(PASSES):
             nc.sync.dma_start(out=w_raw[:, g], in_=w_view[g])
         for b in range(2, BLOCKS):
@@ -90,14 +99,15 @@ def tile_efficientcrossattention_pa_kernel(tc, x, ln_w, ln_b, q_w, q_b, out):
         w_codes = const.tile([P, PASSES, A], U32, align_bytes=64)
         w_scales = const.tile([P, PASSES, A], U8, align_bytes=64)
 
+        def regroup_weights(copy, g):
+            for n in range(HALVES):
+                cols = slice(n * BANK, (n + 1) * BANK)
+                copy(
+                    out=w_grouped[:, g, cols, :].rearrange("p (c i) j -> p c j i", i=4),
+                    in_=w_raw[:, g, :, cols].rearrange("p j (c i) -> p c j i", i=4),
+                )
+
         def quantise_weights():
-            for g in range(PASSES):
-                for n in range(HALVES):
-                    cols = slice(n * BANK, (n + 1) * BANK)
-                    nc.vector.tensor_copy(
-                        out=w_grouped[:, g, cols, :].rearrange("p (c i) j -> p c j i", i=4),
-                        in_=w_raw[:, g, :, cols].rearrange("p j (c i) -> p c j i", i=4),
-                    )
             for g in range(PASSES):
                 for n in range(HALVES):
                     cols = slice(n * BANK, (n + 1) * BANK)
@@ -107,167 +117,186 @@ def tile_efficientcrossattention_pa_kernel(tc, x, ln_w, ln_b, q_w, q_b, out):
                         in_=w_grouped[:, g, cols, :].rearrange("p n j -> p (n j)"),
                     )
 
+        stat_tiles = {}
+        mean_vars = {}
         moments = {}
         x_hats = {}
-        groupeds = {}
+        plane_tiles = {}
+        grouped_tiles = {}
         operands = {}
         accs = {}
         logit_tiles = {}
+        neg_maxes = {}
         expo_tiles = {}
+        inverse_sums = {}
 
-        def stats(b):
-            mean_var = small.tile([P, SUBTILES, 2], F32)
-            for i in range(SUBTILES):
-                stat = small.tile([P, (D // STAT_COLS) * STAT_DIM], F32)
-                for h in range(D // STAT_COLS):
-                    nc.vector.bn_stats(
-                        out=stat[:, h * STAT_DIM : (h + 1) * STAT_DIM],
-                        in_=x_tiles[b][:, i, h * STAT_COLS : (h + 1) * STAT_COLS],
+        def partial_stats(t):
+            stat = small.tile([P, (D // STAT_COLS) * STAT_DIM], F32)
+            for h in range(D // STAT_COLS):
+                nc.vector.bn_stats(
+                    out=stat[:, h * STAT_DIM : (h + 1) * STAT_DIM],
+                    in_=x_tiles[t // SUBTILES][:, t % SUBTILES, h * STAT_COLS : (h + 1) * STAT_COLS],
+                )
+            stat_tiles[t] = stat
+
+        def aggregate(t):
+            if t % SUBTILES == 0:
+                mean_var = small.tile([P, SUBTILES, 2], F32)
+                mean_vars[t // SUBTILES] = mean_var
+            nc.vector.bn_aggr(out=mean_vars[t // SUBTILES][:, t % SUBTILES, :], in_=stat_tiles[t][:])
+
+        def finish_moments(t):
+            if t % SUBTILES == SUBTILES - 1:
+                mean_var = mean_vars[t // SUBTILES]
+                neg_mean = small.tile([P, SUBTILES], F32)
+                nc.vector.tensor_scalar_mul(out=neg_mean[:], in0=mean_var[:, :, 0], scalar1=-1.0)
+                var_eps = small.tile([P, SUBTILES], F32)
+                nc.vector.tensor_scalar_add(out=var_eps[:], in0=mean_var[:, :, 1], scalar1=EPS)
+                rstd = small.tile([P, SUBTILES], F32)
+                nc.gpsimd.tensor_tensor(out=rstd[:], in0=var_eps[:], in1=neg_half[:], op=ALU.pow)
+                moments[t // SUBTILES] = (neg_mean, rstd)
+
+        def centre(t):
+            neg_mean, rstd = moments[t // SUBTILES]
+            i = t % SUBTILES
+            x_hat = hat_pool.tile([P, D], F32)
+            nc.gpsimd.tensor_scalar(
+                out=x_hat[:],
+                in0=x_tiles[t // SUBTILES][:, i, :],
+                scalar1=neg_mean[:, i : i + 1],
+                scalar2=rstd[:, i : i + 1],
+                op0=ALU.add,
+                op1=ALU.mult,
+            )
+            x_hats[t] = x_hat
+
+        def transpose_affine(v):
+            b, g = v // PASSES, v % PASSES
+            planes = norm_pool.tile([P, PACK, BLOCK], BF16)
+            for j in range(PACK):
+                c = g * PACK + j
+                bank = psum_t.tile([P, BANK], F32, tag="bank")
+                for i in range(SUBTILES):
+                    nc.tensor.transpose(
+                        bank[:, i * P : (i + 1) * P], x_hats[b * SUBTILES + i][:, c * P : (c + 1) * P], ident[:]
                     )
-                nc.vector.bn_aggr(out=mean_var[:, i, :], in_=stat[:])
-            neg_mean = small.tile([P, SUBTILES], F32)
-            nc.vector.tensor_scalar_mul(out=neg_mean[:], in0=mean_var[:, :, 0], scalar1=-1.0)
-            var_eps = small.tile([P, SUBTILES], F32)
-            nc.vector.tensor_scalar_add(out=var_eps[:], in0=mean_var[:, :, 1], scalar1=EPS)
-            rstd = small.tile([P, SUBTILES], F32)
-            nc.gpsimd.tensor_tensor(out=rstd[:], in0=var_eps[:], in1=neg_half[:], op=ALU.pow)
-            moments[b] = (neg_mean, rstd)
+                nc.scalar.activation(
+                    out=planes[:, j, :],
+                    in_=bank[:, 0:BLOCK],
+                    func=ACT.Identity,
+                    scale=affine[:, c : c + 1],
+                    bias=affine[:, CHUNKS + c : CHUNKS + c + 1],
+                )
+            plane_tiles[v] = planes
 
-        def centre(b):
-            neg_mean, rstd = moments[b]
-            x_hat = norm_pool.tile([P, SUBTILES, D], F32)
-            for i in range(SUBTILES):
+        def regroup(v):
+            grouped = norm_pool.tile([P, BLOCK, PACK], BF16, align_bytes=64)
+            nc.scalar.copy(
+                out=grouped[:].rearrange("p (c i) j -> p c j i", i=4),
+                in_=plane_tiles[v][:].rearrange("p j (c i) -> p c j i", i=4),
+            )
+            grouped_tiles[v] = grouped
+
+        def quantise(v):
+            x_codes = code_pool.tile([P, BLOCK], U32, align_bytes=64)
+            x_scales = code_pool.tile([P, BLOCK], U8, align_bytes=64)
+            nc.vector.quantize_mx(
+                out=x_codes[:].bitcast(FP8X4),
+                scales=x_scales[:],
+                in_=grouped_tiles[v][:].rearrange("p t j -> p (t j)"),
+            )
+            operands[v] = (x_codes, x_scales)
+
+        def matmuls(t):
+            b, i = t // SUBTILES, t % SUBTILES
+            tok = slice(i * P, (i + 1) * P)
+            for n in range(HALVES):
+                cols = slice(n * BANK, (n + 1) * BANK)
+                acc = psum_q.tile([P, BANK], F32)
+                for g in range(PASSES):
+                    x_codes, x_scales = operands[b * PASSES + g]
+                    nc.tensor.matmul_mx(
+                        out=acc[:],
+                        lhsT=x_codes[:, tok].bitcast(FP8X4),
+                        lhsT_scale=x_scales[:, tok],
+                        rhs=w_codes[:, g, cols].bitcast(FP8X4),
+                        rhs_scale=w_scales[:, g, cols],
+                        start=(g == 0),
+                        stop=(g == PASSES - 1),
+                    )
+                accs[(t, n)] = acc
+
+        def add_bias(t):
+            logits = soft_pool.tile([P, A], F32)
+            for n in range(HALVES):
+                cols = slice(n * BANK, (n + 1) * BANK)
+                nc.vector.tensor_tensor(out=logits[:, cols], in0=accs[(t, n)][:], in1=bias_bc[:, cols], op=ALU.add)
+            logit_tiles[t] = logits
+
+        def row_max(t):
+            neg_max = small.tile([P, HEADS], F32)
+            nc.vector.tensor_reduce(
+                out=neg_max[:],
+                in_=logit_tiles[t][:].rearrange("p (h d) -> p h d", h=HEADS),
+                axis=AXIS.X,
+                op=ALU.max,
+                negate=True,
+            )
+            neg_maxes[t] = neg_max
+
+        def exponentials(t):
+            expo = soft_pool.tile([P, A], F32)
+            sums = small.tile([P, HEADS], F32)
+            for h in range(HEADS):
+                head = slice(h * HEAD_COLS, (h + 1) * HEAD_COLS)
+                nc.scalar.activation(
+                    out=expo[:, head],
+                    in_=logit_tiles[t][:, head],
+                    func=ACT.Exp,
+                    bias=neg_maxes[t][:, h : h + 1],
+                    scale=1.0,
+                    accum_out=sums[:, h : h + 1],
+                )
+            expo_tiles[t] = (expo, sums)
+
+        def invert_sums(t):
+            inv_sums = small.tile([P, HEADS], F32)
+            nc.vector.reciprocal(out=inv_sums[:], in_=expo_tiles[t][1][:])
+            inverse_sums[t] = inv_sums
+
+        def scale_store(t):
+            probs = soft_pool.tile([P, A], F32)
+            for h in range(HEADS):
+                head = slice(h * HEAD_COLS, (h + 1) * HEAD_COLS)
                 nc.gpsimd.tensor_scalar(
-                    out=x_hat[:, i, :],
-                    in0=x_tiles[b][:, i, :],
-                    scalar1=neg_mean[:, i : i + 1],
-                    scalar2=rstd[:, i : i + 1],
-                    op0=ALU.add,
+                    out=probs[:, head],
+                    in0=expo_tiles[t][0][:, head],
+                    scalar1=inverse_sums[t][:, h : h + 1],
+                    scalar2=1.0,
+                    op0=ALU.mult,
                     op1=ALU.mult,
                 )
-            x_hats[b] = x_hat
+            nc.sync.dma_start(out=out_blocks[t // SUBTILES][:, t % SUBTILES, :], in_=probs[:])
 
-        def transpose_affine(b):
-            x_hat = x_hats[b]
-            planes = norm_pool.tile([P, CHUNKS, BLOCK], BF16)
-            grouped = norm_pool.tile([P, PASSES, BLOCK, PACK], BF16, align_bytes=64)
-            for g in range(PASSES):
-                for j in range(PACK):
-                    c = g * PACK + j
-                    bank = psum_t.tile([P, BANK], F32, tag="bank")
-                    for i in range(SUBTILES):
-                        nc.tensor.transpose(
-                            bank[:, i * P : (i + 1) * P], x_hat[:, i, c * P : (c + 1) * P], ident[:]
-                        )
-                    nc.scalar.activation(
-                        out=planes[:, c, :],
-                        in_=bank[:, 0:BLOCK],
-                        func=ACT.Identity,
-                        scale=affine[:, c : c + 1],
-                        bias=affine[:, CHUNKS + c : CHUNKS + c + 1],
-                    )
-                nc.scalar.copy(
-                    out=grouped[:, g].rearrange("p (c i) j -> p c j i", i=4),
-                    in_=planes[:, g * PACK : (g + 1) * PACK, :].rearrange("p j (c i) -> p c j i", i=4),
-                )
-            groupeds[b] = grouped
+        def run(stage, index):
+            if 0 <= index < TILES:
+                stage(index)
 
-        def quantise(b):
-            grouped = groupeds[b]
-            x_codes = norm_pool.tile([P, PASSES, BLOCK], U32, align_bytes=64)
-            x_scales = norm_pool.tile([P, PASSES, BLOCK], U8, align_bytes=64)
-            for g in range(PASSES):
-                nc.vector.quantize_mx(
-                    out=x_codes[:, g, :].bitcast(FP8X4),
-                    scales=x_scales[:, g, :],
-                    in_=grouped[:, g].rearrange("p t j -> p (t j)"),
-                )
-            operands[b] = (x_codes, x_scales)
-
-        def matmuls(b):
-            x_codes, x_scales = operands[b]
-            for i in range(SUBTILES):
-                tok = slice(i * P, (i + 1) * P)
-                for n in range(HALVES):
-                    cols = slice(n * BANK, (n + 1) * BANK)
-                    acc = psum_q.tile([P, BANK], F32)
-                    for g in range(PASSES):
-                        nc.tensor.matmul_mx(
-                            out=acc[:],
-                            lhsT=x_codes[:, g, tok].bitcast(FP8X4),
-                            lhsT_scale=x_scales[:, g, tok],
-                            rhs=w_codes[:, g, cols].bitcast(FP8X4),
-                            rhs_scale=w_scales[:, g, cols],
-                            start=(g == 0),
-                            stop=(g == PASSES - 1),
-                        )
-                    accs[(b, i, n)] = acc
-
-        def bias_max(b):
-            for i in range(SUBTILES):
-                logits = soft_pool.tile([P, A], F32)
-                for n in range(HALVES):
-                    cols = slice(n * BANK, (n + 1) * BANK)
-                    nc.vector.tensor_tensor(
-                        out=logits[:, cols], in0=accs[(b, i, n)][:], in1=bias_bc[:, cols], op=ALU.add
-                    )
-                neg_max = small.tile([P, HEADS], F32)
-                nc.vector.tensor_reduce(
-                    out=neg_max[:],
-                    in_=logits[:].rearrange("p (h d) -> p h d", h=HEADS),
-                    axis=AXIS.X,
-                    op=ALU.max,
-                    negate=True,
-                )
-                logit_tiles[(b, i)] = (logits, neg_max)
-
-        def exponentials(b):
-            for i in range(SUBTILES):
-                logits, neg_max = logit_tiles[(b, i)]
-                expo = soft_pool.tile([P, A], F32)
-                sums = small.tile([P, HEADS], F32)
-                for h in range(HEADS):
-                    head = slice(h * HEAD_COLS, (h + 1) * HEAD_COLS)
-                    nc.scalar.activation(
-                        out=expo[:, head],
-                        in_=logits[:, head],
-                        func=ACT.Exp,
-                        bias=neg_max[:, h : h + 1],
-                        scale=1.0,
-                        accum_out=sums[:, h : h + 1],
-                    )
-                expo_tiles[(b, i)] = (expo, sums)
-
-        def finish(b):
-            for i in range(SUBTILES):
-                expo, sums = expo_tiles[(b, i)]
-                inv_sums = small.tile([P, HEADS], F32)
-                nc.vector.reciprocal(out=inv_sums[:], in_=sums[:])
-                probs = soft_pool.tile([P, A], F32)
-                for h in range(HEADS):
-                    head = slice(h * HEAD_COLS, (h + 1) * HEAD_COLS)
-                    nc.gpsimd.tensor_scalar(
-                        out=probs[:, head],
-                        in0=expo[:, head],
-                        scalar1=inv_sums[:, h : h + 1],
-                        scalar2=1.0,
-                        op0=ALU.mult,
-                        op1=ALU.mult,
-                    )
-                nc.sync.dma_start(out=out_blocks[b][:, i, :], in_=probs[:])
-
-        def run(stage, b):
-            if 0 <= b < BLOCKS:
-                stage(b)
-
-        for step in range(-LEAD_STATS, BLOCKS + 1):
-            if step == WEIGHTS_BEFORE_STEP:
+        regroup_weights(nc.scalar.copy, 0)
+        for step in range(-LEAD_STATS, TILES + LAG_SCALE):
+            if step == WEIGHTS_STEP:
+                regroup_weights(nc.vector.tensor_copy, 1)
                 quantise_weights()
+            run(quantise, step + LEAD_QUANTISE)
+            run(invert_sums, step - LAG_SCALE)
+            run(add_bias, step + LEAD_BIAS)
+            run(aggregate, step + LEAD_MOMENTS)
+            run(row_max, step)
+            run(partial_stats, step + LEAD_STATS)
+            run(finish_moments, step + LEAD_MOMENTS)
             run(transpose_affine, step + LEAD_TRANSPOSE)
-            run(centre, step + LEAD_CENTRE)
-            run(quantise, step + LEAD_MATMUL)
             run(matmuls, step + LEAD_MATMUL)
-            run(bias_max, step)
-            run(exponentials, step)
-            run(finish, step - 1)
-            run(stats, step + LEAD_STATS)
+            run(exponentials, step - LAG_EXP)
+            run(regroup, step + LEAD_TRANSPOSE)
+            run(centre, step + LEAD_CENTRE)
+            run(scale_store, step - LAG_SCALE)

@@ -268,13 +268,10 @@ def tile_efficientcrossattention_pa_kernel(tc, x, ln_w, ln_b, q_w, q_b, out):
             probs = soft_pool.tile([P, A], F32)
             for h in range(HEADS):
                 head = slice(h * HEAD_COLS, (h + 1) * HEAD_COLS)
-                nc.gpsimd.tensor_scalar(
+                nc.vector.tensor_scalar_mul(
                     out=probs[:, head],
                     in0=expo_tiles[t][0][:, head],
                     scalar1=inverse_sums[t][:, h : h + 1],
-                    scalar2=1.0,
-                    op0=ALU.mult,
-                    op1=ALU.mult,
                 )
             nc.sync.dma_start(out=out_blocks[t // SUBTILES][:, t % SUBTILES, :], in_=probs[:])
 
@@ -290,6 +287,7 @@ def tile_efficientcrossattention_pa_kernel(tc, x, ln_w, ln_b, q_w, q_b, out):
             run(quantise, step + LEAD_QUANTISE)
             run(invert_sums, step - LAG_SCALE)
             run(add_bias, step + LEAD_BIAS)
+            run(scale_store, step - LAG_SCALE)
             run(aggregate, step + LEAD_MOMENTS)
             run(row_max, step)
             run(partial_stats, step + LEAD_STATS)
@@ -299,4 +297,3 @@ def tile_efficientcrossattention_pa_kernel(tc, x, ln_w, ln_b, q_w, q_b, out):
             run(exponentials, step - LAG_EXP)
             run(regroup, step + LEAD_TRANSPOSE)
             run(centre, step + LEAD_CENTRE)
-            run(scale_store, step - LAG_SCALE)

@@ -129,6 +129,7 @@ def tile_efficientcrossattention_pa_kernel(tc, x, ln_w, ln_b, q_w, q_b, out):
         neg_maxes = {}
         expo_tiles = {}
         inverse_sums = {}
+        prob_tiles = {}
 
         def partial_stats(t):
             stat = small.tile([P, (D // STAT_COLS) * STAT_DIM], F32)
@@ -264,14 +265,26 @@ def tile_efficientcrossattention_pa_kernel(tc, x, ln_w, ln_b, q_w, q_b, out):
             nc.vector.reciprocal(out=inv_sums[:], in_=expo_tiles[t][1][:])
             inverse_sums[t] = inv_sums
 
-        def scale_store(t):
+        def scale_on_vector(t):
             probs = soft_pool.tile([P, A], F32)
-            for h in range(HEADS):
+            for h in range(HEADS // 2):
                 head = slice(h * HEAD_COLS, (h + 1) * HEAD_COLS)
                 nc.vector.tensor_scalar_mul(
                     out=probs[:, head],
                     in0=expo_tiles[t][0][:, head],
                     scalar1=inverse_sums[t][:, h : h + 1],
+                )
+            prob_tiles[t] = probs
+
+        def scale_on_scalar_store(t):
+            probs = prob_tiles[t]
+            for h in range(HEADS // 2, HEADS):
+                head = slice(h * HEAD_COLS, (h + 1) * HEAD_COLS)
+                nc.scalar.activation(
+                    out=probs[:, head],
+                    in_=expo_tiles[t][0][:, head],
+                    func=ACT.Copy,
+                    scale=inverse_sums[t][:, h : h + 1],
                 )
             nc.sync.dma_start(out=out_blocks[t // SUBTILES][:, t % SUBTILES, :], in_=probs[:])
 
@@ -287,7 +300,7 @@ def tile_efficientcrossattention_pa_kernel(tc, x, ln_w, ln_b, q_w, q_b, out):
             run(quantise, step + LEAD_QUANTISE)
             run(invert_sums, step - LAG_SCALE)
             run(add_bias, step + LEAD_BIAS)
-            run(scale_store, step - LAG_SCALE)
+            run(scale_on_vector, step - LAG_SCALE)
             run(aggregate, step + LEAD_MOMENTS)
             run(row_max, step)
             run(partial_stats, step + LEAD_STATS)
@@ -295,5 +308,6 @@ def tile_efficientcrossattention_pa_kernel(tc, x, ln_w, ln_b, q_w, q_b, out):
             run(transpose_affine, step + LEAD_TRANSPOSE)
             run(matmuls, step + LEAD_MATMUL)
             run(exponentials, step - LAG_EXP)
+            run(scale_on_scalar_store, step - LAG_SCALE)
             run(regroup, step + LEAD_TRANSPOSE)
             run(centre, step + LEAD_CENTRE)

@@ -161,7 +161,8 @@ def tile_efficientcrossattention_pa_kernel(tc, x, ln_w, ln_b, q_w, q_b, out):
             neg_mean, rstd = moments[t // SUBTILES]
             i = t % SUBTILES
             x_hat = hat_pool.tile([P, D], F32)
-            nc.gpsimd.tensor_scalar(
+            engine = nc.gpsimd if t % 2 == 0 else nc.vector
+            engine.tensor_scalar(
                 out=x_hat[:],
                 in0=x_tiles[t // SUBTILES][:, i, :],
                 scalar1=neg_mean[:, i : i + 1],

from contextlib import ExitStack

import concourse.mybir as mybir
from concourse.masks import make_identity

F32 = mybir.dt.float32
BF16 = mybir.dt.bfloat16
U32 = mybir.dt.uint32
U8 = mybir.dt.uint8
FP8X4 = mybir.dt.float8_e4m3fn_x4
ALU = mybir.AluOpType
ACT = mybir.ActivationFunctionType
AXIS = mybir.AxisListType

P = 128
TOKENS = 4 * 512
D = 1024
A = 1024
HEADS = 4
HEAD_COLS = A // HEADS
EPS = 1e-5

PACK = 4
K_PASS = P * PACK
PASSES = D // K_PASS
CHUNKS = D // P
TILES = TOKENS // P
SUBTILES = 2
BLOCK = P * SUBTILES
BLOCKS = TOKENS // BLOCK
BANK = 512
HALVES = A // BANK
STAT_COLS = 512
STAT_DIM = 6

assert SUBTILES == PASSES
LEAD_STATS = 10
LEAD_MOMENTS = 9
LEAD_CENTRE = 8
LEAD_TRANSPOSE = 5
LEAD_QUANTISE = 3
LEAD_MATMUL = 2
LEAD_BIAS = 1
LAG_EXP = 1
LAG_SCALE = 2
WEIGHTS_STEP = -4

FLOPS = 2 * TOKENS * D * A


def tile_efficientcrossattention_pa_kernel(tc, x, ln_w, ln_b, q_w, q_b, out):
    nc = tc.nc
    x_blocks = x.flatten_outer_dims().rearrange("(b p i) k -> b p i k", p=P, i=SUBTILES)
    out_blocks = out.flatten_outer_dims().rearrange("(b p i) a -> b p i a", p=P, i=SUBTILES)

    with ExitStack() as ctx:
        const = ctx.enter_context(tc.tile_pool(name="const", bufs=1))
        x_pool = ctx.enter_context(tc.tile_pool(name="x", bufs=BLOCKS))
        hat_pool = ctx.enter_context(tc.tile_pool(name="hat", bufs=6))
        norm_pool = ctx.enter_context(tc.tile_pool(name="norm", bufs=4))
        code_pool = ctx.enter_context(tc.tile_pool(name="code", bufs=6))
        small = ctx.enter_context(tc.tile_pool(name="small", bufs=16))
        soft_pool = ctx.enter_context(tc.tile_pool(name="soft", bufs=4))
        psum_t = ctx.enter_context(tc.psum_pool(name="psum_t", bufs=4))
        psum_q = ctx.enter_context(tc.psum_pool(name="psum_q", bufs=4))
        ctx.enter_context(tc.manual_schedule())

        rows_bf = const.tile([P, P], BF16)
        nc.vector.memset(rows_bf[:], 0.0)
        nc.sync.dma_start(out=rows_bf[0:CHUNKS, :], in_=ln_w.rearrange("(c p) -> c p", p=P))
        nc.sync.dma_start(out=rows_bf[CHUNKS : 2 * CHUNKS, :], in_=ln_b.rearrange("(c p) -> c p", p=P))
        x_tiles = []
        for b in range(BLOCKS):
            x_blk = x_pool.tile([P, SUBTILES, D], BF16)
            x_tiles.append(x_blk)
        for b in range(2):
            nc.sync.dma_start(out=x_tiles[b][:], in_=x_blocks[b])
        bias_bc = const.tile([P, A], BF16)
        nc.sync.dma_start(out=bias_bc[:], in_=q_b.partition_broadcast(P))
        w_raw = const.tile([P, PASSES, PACK, A], BF16)
        w_view = q_w.rearrange("(g j p) n -> g p j n", j=PACK, p=P)
        for g in range(PASSES):
            nc.sync.dma_start(out=w_raw[:, g], in_=w_view[g])
        for b in range(2, BLOCKS):
            nc.sync.dma_start(out=x_tiles[b][:], in_=x_blocks[b])

        ident = const.tile([P, P], F32)
        make_identity(nc, ident[:])
        neg_half = const.tile([P, SUBTILES], F32)
        nc.vector.memset(neg_half[:], -0.5)
        rows_f = const.tile([P, P], F32)
        nc.vector.tensor_copy(out=rows_f[:], in_=rows_bf[:])
        rows_t = psum_t.tile([P, BANK], F32, tag="bank")
        nc.tensor.transpose(rows_t[:, 0:P], rows_f[:], ident[:])
        affine = const.tile([P, 2 * CHUNKS], F32)
        nc.vector.tensor_copy(out=affine[:], in_=rows_t[:, 0 : 2 * CHUNKS])

        w_grouped = const.tile([P, PASSES, A, PACK], BF16, align_bytes=64)
        w_codes = const.tile([P, PASSES, A], U32, align_bytes=64)
        w_scales = const.tile([P, PASSES, A], U8, align_bytes=64)

        def regroup_weights(copy, g):
            for n in range(HALVES):
                cols = slice(n * BANK, (n + 1) * BANK)
                copy(
                    out=w_grouped[:, g, cols, :].rearrange("p (c i) j -> p c j i", i=4),
                    in_=w_raw[:, g, :, cols].rearrange("p j (c i) -> p c j i", i=4),
                )

        def quantise_weights():
            for g in range(PASSES):
                for n in range(HALVES):
                    cols = slice(n * BANK, (n + 1) * BANK)
                    nc.vector.quantize_mx(
                        out=w_codes[:, g, cols].bitcast(FP8X4),
                        scales=w_scales[:, g, cols],
                        in_=w_grouped[:, g, cols, :].rearrange("p n j -> p (n j)"),
                    )

        stat_tiles = {}
        mean_vars = {}
        moments = {}
        x_hats = {}
        plane_tiles = {}
        grouped_tiles = {}
        operands = {}
        accs = {}
        logit_tiles = {}
        neg_maxes = {}
        expo_tiles = {}
        inverse_sums = {}
        prob_tiles = {}

        def partial_stats(t):
            stat = small.tile([P, (D // STAT_COLS) * STAT_DIM], F32)
            for h in range(D // STAT_COLS):
                nc.vector.bn_stats(
                    out=stat[:, h * STAT_DIM : (h + 1) * STAT_DIM],
                    in_=x_tiles[t // SUBTILES][:, t % SUBTILES, h * STAT_COLS : (h + 1) * STAT_COLS],
                )
            stat_tiles[t] = stat

        def aggregate(t):
            if t % SUBTILES == 0:
                mean_var = small.tile([P, SUBTILES, 2], F32)
                mean_vars[t // SUBTILES] = mean_var
            nc.vector.bn_aggr(out=mean_vars[t // SUBTILES][:, t % SUBTILES, :], in_=stat_tiles[t][:])

        def finish_moments(t):
            if t % SUBTILES == SUBTILES - 1:
                mean_var = mean_vars[t // SUBTILES]
                neg_mean = small.tile([P, SUBTILES], F32)
                nc.vector.tensor_scalar_mul(out=neg_mean[:], in0=mean_var[:, :, 0], scalar1=-1.0)
                var_eps = small.tile([P, SUBTILES], F32)
                nc.vector.tensor_scalar_add(out=var_eps[:], in0=mean_var[:, :, 1], scalar1=EPS)
                rstd = small.tile([P, SUBTILES], F32)
                nc.gpsimd.tensor_tensor(out=rstd[:], in0=var_eps[:], in1=neg_half[:], op=ALU.pow)
                moments[t // SUBTILES] = (neg_mean, rstd)

        def centre(t):
            neg_mean, rstd = moments[t // SUBTILES]
            i = t % SUBTILES
            x_hat = hat_pool.tile([P, D], F32)
            engine = nc.gpsimd if t % 2 == 0 else nc.vector
            engine.tensor_scalar(
                out=x_hat[:],
                in0=x_tiles[t // SUBTILES][:, i, :],
                scalar1=neg_mean[:, i : i + 1],
                scalar2=rstd[:, i : i + 1],
                op0=ALU.add,
                op1=ALU.mult,
            )
            x_hats[t] = x_hat

        def transpose_affine(v):
            b, g = v // PASSES, v % PASSES
            planes = norm_pool.tile([P, PACK, BLOCK], BF16)
            for j in range(PACK):
                c = g * PACK + j
                bank = psum_t.tile([P, BANK], F32, tag="bank")
                for i in range(SUBTILES):
                    nc.tensor.transpose(
                        bank[:, i * P : (i + 1) * P], x_hats[b * SUBTILES + i][:, c * P : (c + 1) * P], ident[:]
                    )
                nc.scalar.activation(
                    out=planes[:, j, :],
                    in_=bank[:, 0:BLOCK],
                    func=ACT.Identity,
                    scale=affine[:, c : c + 1],
                    bias=affine[:, CHUNKS + c : CHUNKS + c + 1],
                )
            plane_tiles[v] = planes

        def regroup(v):
            grouped = norm_pool.tile([P, BLOCK, PACK], BF16, align_bytes=64)
            nc.scalar.copy(
                out=grouped[:].rearrange("p (c i) j -> p c j i", i=4),
                in_=plane_tiles[v][:].rearrange("p j (c i) -> p c j i", i=4),
            )
            grouped_tiles[v] = grouped

        def quantise(v):
            x_codes = code_pool.tile([P, BLOCK], U32, align_bytes=64)
            x_scales = code_pool.tile([P, BLOCK], U8, align_bytes=64)
            nc.vector.quantize_mx(
                out=x_codes[:].bitcast(FP8X4),
                scales=x_scales[:],
                in_=grouped_tiles[v][:].rearrange("p t j -> p (t j)"),
            )
            operands[v] = (x_codes, x_scales)

        def matmuls(t):
            b, i = t // SUBTILES, t % SUBTILES
            tok = slice(i * P, (i + 1) * P)
            for n in range(HALVES):
                cols = slice(n * BANK, (n + 1) * BANK)
                acc = psum_q.tile([P, BANK], F32)
                for g in range(PASSES):
                    x_codes, x_scales = operands[b * PASSES + g]
                    nc.tensor.matmul_mx(
                        out=acc[:],
                        lhsT=x_codes[:, tok].bitcast(FP8X4),
                        lhsT_scale=x_scales[:, tok],
                        rhs=w_codes[:, g, cols].bitcast(FP8X4),
                        rhs_scale=w_scales[:, g, cols],
                        start=(g == 0),
                        stop=(g == PASSES - 1),
                    )
                accs[(t, n)] = acc

        def add_bias(t):
            logits = soft_pool.tile([P, A], F32)
            for n in range(HALVES):
                cols = slice(n * BANK, (n + 1) * BANK)
                nc.vector.tensor_tensor(out=logits[:, cols], in0=accs[(t, n)][:], in1=bias_bc[:, cols], op=ALU.add)
            logit_tiles[t] = logits

        def row_max(t):
            neg_max = small.tile([P, HEADS], F32)
            nc.vector.tensor_reduce(
                out=neg_max[:],
                in_=logit_tiles[t][:].rearrange("p (h d) -> p h d", h=HEADS),
                axis=AXIS.X,
                op=ALU.max,
                negate=True,
            )
            neg_maxes[t] = neg_max

        def exponentials(t):
            expo = soft_pool.tile([P, A], F32)
            sums = small.tile([P, HEADS], F32)
            for h in range(HEADS):
                head = slice(h * HEAD_COLS, (h + 1) * HEAD_COLS)
                nc.scalar.activation(
                    out=expo[:, head],
                    in_=logit_tiles[t][:, head],
                    func=ACT.Exp,
                    bias=neg_maxes[t][:, h : h + 1],
                    scale=1.0,
                    accum_out=sums[:, h : h + 1],
                )
            expo_tiles[t] = (expo, sums)

        def invert_sums(t):
            inv_sums = small.tile([P, HEADS], F32)
            nc.vector.reciprocal(out=inv_sums[:], in_=expo_tiles[t][1][:])
            inverse_sums[t] = inv_sums

        def scale_on_vector(t):
            probs = soft_pool.tile([P, A], F32)
            for h in range(HEADS // 2):
                head = slice(h * HEAD_COLS, (h + 1) * HEAD_COLS)
                nc.vector.tensor_scalar_mul(
                    out=probs[:, head],
                    in0=expo_tiles[t][0][:, head],
                    scalar1=inverse_sums[t][:, h : h + 1],
                )
            prob_tiles[t] = probs

        def scale_on_scalar_store(t):
            probs = prob_tiles[t]
            for h in range(HEADS // 2, HEADS):
                head = slice(h * HEAD_COLS, (h + 1) * HEAD_COLS)
                nc.scalar.activation(
                    out=probs[:, head],
                    in_=expo_tiles[t][0][:, head],
                    func=ACT.Copy,
                    scale=inverse_sums[t][:, h : h + 1],
                )
            nc.sync.dma_start(out=out_blocks[t // SUBTILES][:, t % SUBTILES, :], in_=probs[:])

        def run(stage, index):
            if 0 <= index < TILES:
                stage(index)

        regroup_weights(nc.scalar.copy, 0)
        for step in range(-LEAD_STATS, TILES + LAG_SCALE):
            if step == WEIGHTS_STEP:
                regroup_weights(nc.vector.tensor_copy, 1)
                quantise_weights()
            run(quantise, step + LEAD_QUANTISE)
            run(invert_sums, step - LAG_SCALE)
            run(add_bias, step + LEAD_BIAS)
            run(scale_on_vector, step - LAG_SCALE)
            run(aggregate, step + LEAD_MOMENTS)
            run(row_max, step)
            run(partial_stats, step + LEAD_STATS)
            run(finish_moments, step + LEAD_MOMENTS)
            run(transpose_affine, step + LEAD_TRANSPOSE)
            run(matmuls, step + LEAD_MATMUL)
            run(exponentials, step - LAG_EXP)
            run(scale_on_scalar_store, step - LAG_SCALE)
            run(regroup, step + LEAD_TRANSPOSE)
            run(centre, step + LEAD_CENTRE)
